import numpy as np
import ml_dtypes


def mxq(x, axis, fmt="e4m3"):
    dtype, down = {"e4m3": (ml_dtypes.float8_e4m3fn, 7), "e5m2": (ml_dtypes.float8_e5m2, 14)}[fmt]
    v = np.moveaxis(np.asarray(x, np.float32).astype(ml_dtypes.bfloat16).astype(np.float64), axis, -1)
    blocks = v.reshape(v.shape[:-1] + (-1, 32))
    amax = np.abs(blocks).max(-1, keepdims=True)
    byte = np.maximum(np.where(amax > 0, np.frexp(amax)[1] - 1 + 127, 0) - down, 1)
    scale = np.exp2(byte - 127.0)
    codes = (blocks / scale).astype(np.float32).astype(dtype).astype(np.float64)
    return np.moveaxis((codes * scale).reshape(v.shape), -1, axis)


WIDE = False


def mx_kscale(k):
    if not WIDE:
        return np.ones(k)
    levels = np.array([10, -10, 5, -5, 0])
    if k % 512:
        return np.exp2(np.random.permutation(np.resize(levels, k // 32))).repeat(32)
    a = np.empty((k // 512, 16))
    for p in range(k // 512):
        a[p, :8] = np.random.permutation(np.resize(levels, 8))
        for g in range(8):
            far = levels[np.abs(levels - a[p, g]) >= 10]
            a[p, g + 8] = far[np.random.randint(len(far))]
    return np.exp2(a.ravel()).repeat(32)


BF16 = ml_dtypes.bfloat16


def bf(x):
    return np.asarray(x, np.float32).astype(BF16)


def f64(x):
    return np.asarray(x).astype(np.float64)


T, K, E, H, KVH, D = 512, 1024, 2048, 16, 4, 128
EPS = 1e-05


def rmsnorm(x, w):
    var = np.mean(np.square(x), axis=-1, keepdims=True)
    return x * (1.0 / np.sqrt(var + EPS)) * w


def setup_inputs():
    s = mx_kscale(E)
    return {"hidden_states": bf(np.random.standard_normal((T, E)) * s),
            "Wq": bf(np.random.standard_normal((H * D, E)) / np.sqrt(E) / s),
            "q_norm_w": bf(1.5 + 0.1 * np.random.standard_normal(D))}


def reference(hidden_states, Wq, q_norm_w):
    q = mxq(f64(hidden_states), 1, "e4m3") @ mxq(f64(Wq), 1, "e4m3").T
    qh = rmsnorm(q.reshape(T, H, D), f64(q_norm_w))
    return qh.transpose(1, 0, 2)

@@ -1,0 +1,210 @@
+import concourse.mybir as mybir
+from concourse.masks import make_identity
+
+F32 = mybir.dt.float32
+BF16 = mybir.dt.bfloat16
+U32 = mybir.dt.uint32
+U8 = mybir.dt.uint8
+FP8X4 = mybir.dt.float8_e4m3fn_x4
+ACT = mybir.ActivationFunctionType
+ALU = mybir.AluOpType
+
+P = 128
+TOKENS, EMBED, HEADS, HEAD_DIM = 512, 2048, 16, 128
+EPS = 1e-05
+
+K_PASS = 4 * P
+PASSES = EMBED // K_PASS
+BANK_WORDS = 512
+
+TOKEN_TILES = TOKENS // P
+UNIT_TILES = 2
+UNIT_COLS = UNIT_TILES * P
+UNIT_BANKS = UNIT_TILES * EMBED // 2 // BANK_WORDS
+TOKEN_UNITS = TOKEN_TILES // UNIT_TILES
+WEIGHT_UNITS = HEADS // UNIT_TILES
+
+RESULT_BUFS = TOKEN_UNITS * WEIGHT_UNITS
+
+IDLE_MATMULS_AT_START = 6
+IDLE_MATMULS_A_UNIT = 3
+IDLE_COLS = 512
+
+FLOPS = 2 * TOKENS * EMBED * HEADS * HEAD_DIM
+
+
+def tile_combcrossattention_pa_kernel(tc, hidden_states, Wq, q_norm_w, out):
+    nc = tc.nc
+
+    with (
+        tc.tile_pool(name="consts", bufs=1) as consts,
+        tc.tile_pool(name="raw", bufs=1) as raw_pool,
+        tc.tile_pool(name="quantised", bufs=1) as quantised,
+        tc.tile_pool(name="grouped", bufs=4) as grouped_pool,
+        tc.tile_pool(name="stats", bufs=4) as stats,
+        tc.tile_pool(name="results", bufs=RESULT_BUFS) as results,
+        tc.psum_pool(name="flipped", bufs=UNIT_BANKS) as flipped_pool,
+        tc.psum_pool(name="sums", bufs=TOKEN_TILES) as sums_pool,
+        tc.manual_schedule(),
+    ):
+        tokens_by_partition = hidden_states.rearrange("(p i) k -> p i k", p=P)
+
+        def load_token_unit(r):
+            tiles = []
+            for a in range(UNIT_TILES):
+                raw = raw_pool.tile([P, EMBED], BF16, name="token_raw%d" % (UNIT_TILES * r + a))
+                nc.sync.dma_start(out=raw[:], in_=tokens_by_partition[:, UNIT_TILES * r + a, :])
+                tiles.append(raw)
+            return tiles
+
+        def load_weight_unit(b):
+            tiles = []
+            for a in range(UNIT_TILES):
+                head = UNIT_TILES * b + a
+                raw = raw_pool.tile([P, EMBED], BF16, name="weight_raw%d" % head)
+                nc.sync.dma_start(out=raw[:], in_=Wq[P * head : P * (head + 1), :])
+                tiles.append(raw)
+            return tiles
+
+        token_raw = [load_token_unit(0)]
+        weight_raw = [load_weight_unit(0)]
+        token_raw.append(load_token_unit(1))
+        for b in range(1, WEIGHT_UNITS):
+            weight_raw.append(load_weight_unit(b))
+
+        identity = consts.tile([P, P], F32)
+        make_identity(nc, identity[:])
+        gain_row = consts.tile([P, HEAD_DIM], BF16)
+        nc.vector.memset(gain_row[:], 0.0)
+        nc.scalar.dma_start(out=gain_row[0:1, :], in_=q_norm_w.unsqueeze(0))
+        ones = consts.tile([P, P], BF16)
+        nc.vector.memset(ones[:], 1.0)
+        gain = consts.tile([P, HEAD_DIM], F32)
+        eps = consts.tile([P, 1], F32)
+        nc.vector.memset(eps[:], EPS)
+
+        idle_rhs = consts.tile([P, IDLE_COLS], BF16)
+        nc.vector.memset(idle_rhs[:], 0.0)
+
+        def keep_clock_up(count):
+            unread = sums_pool.tile([P, IDLE_COLS], F32, name="unread", tag="q")
+            for n in range(count):
+                nc.tensor.matmul(out=unread[:], lhsT=ones[:], rhs=idle_rhs[:], start=True, stop=True)
+
+        def spread_gain():
+            bank = flipped_pool.tile([P, 4, P], F32, name="bank")
+            nc.tensor.matmul(out=bank[:, 0, :], lhsT=ones[:], rhs=gain_row[:], start=True, stop=True)
+            nc.vector.tensor_copy(out=gain[:], in_=bank[:, 0, :])
+
+        table_warmer = consts.tile([P, 1], F32)
+        nc.scalar.activation(out=table_warmer[:], in_=eps[:], func=ACT.Abs_reciprocal_sqrt)
+
+        def quantise_unit(raw_tiles, name, unit_number):
+            codes = quantised.tile([P, PASSES, UNIT_COLS], U32, name=name + "_codes", align_bytes=64)
+            scales = quantised.tile([P, PASSES, UNIT_COLS], U8, name=name + "_scales", align_bytes=64)
+
+            banks = []
+            for a in range(UNIT_TILES):
+                words = raw_tiles[a][:].bitcast(F32)
+                for pair in range(PASSES // 2):
+                    bank = flipped_pool.tile([P, 4, P], F32, name="bank")
+                    for s in range(4):
+                        first = BANK_WORDS * pair + 2 * P * (s // 2) + s % 2
+                        nc.tensor.transpose(
+                            bank[:, s, :], words[:, first : first + 2 * P - 1 : 2], identity[:]
+                        )
+                    banks.append((a, pair, bank))
+
+            grouped = []
+            for pair in range(PASSES // 2):
+                grouped.append(grouped_pool.tile([P, 2 * 4 * UNIT_COLS], BF16, name="grouped", align_bytes=64))
+            for n, (a, pair, bank) in enumerate(banks):
+                target = grouped[pair][:].bitcast(F32).rearrange(
+                    "p (g a c u) -> p g a c u", g=2, a=UNIT_TILES, u=2
+                )[:, :, a]
+                source = bank[:].rearrange("p (g u) c -> p g c u", u=2)
+                if (UNIT_BANKS * unit_number + n) % 3 == 2:
+                    nc.vector.tensor_copy(out=target, in_=source)
+                else:
+                    nc.scalar.copy(out=target, in_=source)
+
+            for pair in range(PASSES // 2):
+                two_passes = slice(2 * pair, 2 * pair + 2)
+                nc.vector.quantize_mx(
+                    out=codes[:, two_passes, :].rearrange("p g n -> p (g n)").bitcast(FP8X4),
+                    scales=scales[:, two_passes, :].rearrange("p g n -> p (g n)"),
+                    in_=grouped[pair][:],
+                )
+            return codes, scales
+
+        out_by_partition = out.rearrange("h (p i) d -> p h i d", p=P)
+
+        def product(b, r, weight_unit, token_unit):
+            weight_codes, weight_scales = weight_unit
+            token_codes, token_scales = token_unit
+            groups = []
+            for a in range(UNIT_TILES):
+                cols = slice(P * a, P * (a + 1))
+                q = sums_pool.tile([P, UNIT_COLS], F32, name="q")
+                for g in range(PASSES):
+                    nc.tensor.matmul_mx(
+                        out=q[:],
+                        lhsT=token_codes[:, g, cols].bitcast(FP8X4),
+                        lhsT_scale=token_scales[:, g, cols],
+                        rhs=weight_codes[:, g, :].bitcast(FP8X4),
+                        rhs_scale=weight_scales[:, g, :],
+                        start=(g == 0),
+                        stop=(g == PASSES - 1),
+                    )
+                groups.append(q)
+
+            pieces = [(a, h) for a in range(UNIT_TILES) for h in range(UNIT_TILES)]
+            squares = stats.tile([P, len(pieces), HEAD_DIM], F32, name="squares")
+            sum_squares = stats.tile([P, len(pieces)], F32, name="sum_squares")
+            for n, (a, h) in enumerate(pieces):
+                nc.scalar.activation(
+                    out=squares[:, n, :],
+                    in_=groups[a][:, HEAD_DIM * h : HEAD_DIM * (h + 1)],
+                    func=ACT.Square,
+                    accum_out=sum_squares[:, n : n + 1],
+                )
+            inv_rms = stats.tile([P, len(pieces)], F32, name="inv_rms")
+            nc.scalar.activation(
+                out=inv_rms[:],
+                in_=sum_squares[:],
+                func=ACT.Abs_reciprocal_sqrt,
+                scale=1.0 / HEAD_DIM,
+                bias=eps[:],
+            )
+            result = results.tile([P, UNIT_TILES, UNIT_TILES, HEAD_DIM], F32, name="result")
+            for n, (a, h) in enumerate(pieces):
+                nc.vector.scalar_tensor_tensor(
+                    out=result[:, h, a, :],
+                    in0=groups[a][:, HEAD_DIM * h : HEAD_DIM * (h + 1)],
+                    scalar=inv_rms[:, n : n + 1],
+                    in1=gain[:],
+                    op0=ALU.mult,
+                    op1=ALU.mult,
+                )
+            nc.sync.dma_start(
+                out=out_by_partition[
+                    :, UNIT_TILES * b : UNIT_TILES * (b + 1), UNIT_TILES * r : UNIT_TILES * (r + 1), :
+                ],
+                in_=result[:],
+            )
+
+        keep_clock_up(IDLE_MATMULS_AT_START)
+        token_units = [quantise_unit(token_raw[0], "token0", 0)]
+        keep_clock_up(IDLE_MATMULS_A_UNIT)
+        weight_units = [quantise_unit(weight_raw[0], "weight0", 1)]
+        spread_gain()
+        keep_clock_up(IDLE_MATMULS_A_UNIT)
+        token_units.append(quantise_unit(token_raw[1], "token1", 2))
+        product(0, 0, weight_units[0], token_units[0])
+        weight_units.append(quantise_unit(weight_raw[1], "weight1", 3))
+        product(0, 1, weight_units[0], token_units[1])
+        for b in range(1, WEIGHT_UNITS):
+            if b + 1 < WEIGHT_UNITS:
+                weight_units.append(quantise_unit(weight_raw[b + 1], "weight%d" % (b + 1), b + 3))
+            for r in range(TOKEN_UNITS):
+                product(b, r, weight_units[b], token_units[r])

@@ -15,19 +15,16 @@ EPS = 1e-05
 
 K_PASS = 4 * P
 PASSES = EMBED // K_PASS
-BANK_WORDS = 512
+HALVES = 2
+HALF_PASSES = PASSES // HALVES
+HALF_COLS = EMBED // HALVES
+HALF_WORDS = HALF_COLS // 2
 
 TOKEN_TILES = TOKENS // P
-UNIT_TILES = 2
-UNIT_COLS = UNIT_TILES * P
-UNIT_BANKS = UNIT_TILES * EMBED // 2 // BANK_WORDS
-TOKEN_UNITS = TOKEN_TILES // UNIT_TILES
-WEIGHT_UNITS = HEADS // UNIT_TILES
+UNIT_HEADS = 2
+UNIT_COLS = UNIT_HEADS * P
+WEIGHT_UNITS = HEADS // UNIT_HEADS
 
-RESULT_BUFS = TOKEN_UNITS * WEIGHT_UNITS
-
-IDLE_MATMULS_AT_START = 6
-IDLE_MATMULS_A_UNIT = 3
 IDLE_COLS = 512
 
 FLOPS = 2 * TOKENS * EMBED * HEADS * HEAD_DIM
@@ -39,52 +36,55 @@ def tile_combcrossattention_pa_kernel(tc, hidden_states, Wq, q_norm_w, out):
     with (
         tc.tile_pool(name="consts", bufs=1) as consts,
         tc.tile_pool(name="raw", bufs=1) as raw_pool,
+        tc.tile_pool(name="sorted", bufs=10) as sorted_pool,
         tc.tile_pool(name="quantised", bufs=1) as quantised,
         tc.tile_pool(name="grouped", bufs=4) as grouped_pool,
-        tc.tile_pool(name="stats", bufs=4) as stats,
-        tc.tile_pool(name="results", bufs=RESULT_BUFS) as results,
-        tc.psum_pool(name="flipped", bufs=UNIT_BANKS) as flipped_pool,
-        tc.psum_pool(name="sums", bufs=TOKEN_TILES) as sums_pool,
+        tc.tile_pool(name="stats", bufs=6) as stats,
+        tc.tile_pool(name="results", bufs=8) as results,
+        tc.psum_pool(name="flipped", bufs=4) as flipped_pool,
+        tc.psum_pool(name="sums", bufs=4) as sums_pool,
         tc.manual_schedule(),
     ):
         tokens_by_partition = hidden_states.rearrange("(p i) k -> p i k", p=P)
+        token_raw = []
+        weight_raw = []
 
-        def load_token_unit(r):
-            tiles = []
-            for a in range(UNIT_TILES):
-                raw = raw_pool.tile([P, EMBED], BF16, name="token_raw%d" % (UNIT_TILES * r + a))
-                nc.sync.dma_start(out=raw[:], in_=tokens_by_partition[:, UNIT_TILES * r + a, :])
-                tiles.append(raw)
-            return tiles
+        def load_tokens(i, pieces):
+            raw = raw_pool.tile([P, EMBED], BF16, name="token_raw%d" % i)
+            width = EMBED // pieces
+            for n in range(pieces):
+                cols = slice(width * n, width * (n + 1))
+                nc.sync.dma_start(out=raw[:, cols], in_=tokens_by_partition[:, i, cols])
+            token_raw.append(raw)
 
-        def load_weight_unit(b):
-            tiles = []
-            for a in range(UNIT_TILES):
-                head = UNIT_TILES * b + a
-                raw = raw_pool.tile([P, EMBED], BF16, name="weight_raw%d" % head)
-                nc.sync.dma_start(out=raw[:], in_=Wq[P * head : P * (head + 1), :])
-                tiles.append(raw)
-            return tiles
+        def load_weights(head):
+            raw = raw_pool.tile([P, EMBED], BF16, name="weight_raw%d" % head)
+            nc.sync.dma_start(out=raw[:], in_=Wq[P * head : P * (head + 1), :])
+            weight_raw.append(raw)
 
-        token_raw = [load_token_unit(0)]
-        weight_raw = [load_weight_unit(0)]
-        token_raw.append(load_token_unit(1))
-        for b in range(1, WEIGHT_UNITS):
-            weight_raw.append(load_weight_unit(b))
+        load_tokens(0, 2)
+        load_weights(0)
+        load_weights(1)
+        for i in range(1, TOKEN_TILES):
+            load_tokens(i, 1)
+        for head in range(2, HEADS):
+            load_weights(head)
 
         identity = consts.tile([P, P], F32)
         make_identity(nc, identity[:])
+        ones = consts.tile([P, P], BF16)
+        nc.vector.memset(ones[:], 1.0)
+        idle_rhs = consts.tile([P, IDLE_COLS], BF16)
+        nc.vector.memset(idle_rhs[:], 0.0)
         gain_row = consts.tile([P, HEAD_DIM], BF16)
         nc.vector.memset(gain_row[:], 0.0)
         nc.scalar.dma_start(out=gain_row[0:1, :], in_=q_norm_w.unsqueeze(0))
-        ones = consts.tile([P, P], BF16)
-        nc.vector.memset(ones[:], 1.0)
         gain = consts.tile([P, HEAD_DIM], F32)
         eps = consts.tile([P, 1], F32)
         nc.vector.memset(eps[:], EPS)
 
-        idle_rhs = consts.tile([P, IDLE_COLS], BF16)
-        nc.vector.memset(idle_rhs[:], 0.0)
+        table_warmer = consts.tile([P, 1], F32)
+        nc.scalar.activation(out=table_warmer[:], in_=eps[:], func=ACT.Abs_reciprocal_sqrt)
 
         def keep_clock_up(count):
             unread = sums_pool.tile([P, IDLE_COLS], F32, name="unread", tag="q")
@@ -96,115 +96,241 @@ def tile_combcrossattention_pa_kernel(tc, hidden_states, Wq, q_norm_w, out):
             nc.tensor.matmul(out=bank[:, 0, :], lhsT=ones[:], rhs=gain_row[:], start=True, stop=True)
             nc.vector.tensor_copy(out=gain[:], in_=bank[:, 0, :])
 
-        table_warmer = consts.tile([P, 1], F32)
-        nc.scalar.activation(out=table_warmer[:], in_=eps[:], func=ACT.Abs_reciprocal_sqrt)
+        def sort(raw, h):
+            words = sorted_pool.tile([P, 2, HALF_WORDS // 2], F32, name="words")
+            nc.vector.tensor_copy(
+                out=words[:],
+                in_=raw[:, HALF_COLS * h : HALF_COLS * (h + 1)].bitcast(F32).rearrange("p (w u) -> p u w", u=2),
+            )
+            return words
 
-        def quantise_unit(raw_tiles, name, unit_number):
-            codes = quantised.tile([P, PASSES, UNIT_COLS], U32, name=name + "_codes", align_bytes=64)
-            scales = quantised.tile([P, PASSES, UNIT_COLS], U8, name=name + "_scales", align_bytes=64)
+        def flip(words):
+            bank = flipped_pool.tile([P, 4, P], F32, name="bank")
+            for g in range(HALF_PASSES):
+                for u in range(2):
+                    nc.tensor.transpose(bank[:, 2 * g + u, :], words[:, u, P * g : P * (g + 1)], identity[:])
+            return bank
 
-            banks = []
-            for a in range(UNIT_TILES):
-                words = raw_tiles[a][:].bitcast(F32)
-                for pair in range(PASSES // 2):
-                    bank = flipped_pool.tile([P, 4, P], F32, name="bank")
-                    for s in range(4):
-                        first = BANK_WORDS * pair + 2 * P * (s // 2) + s % 2
-                        nc.tensor.transpose(
-                            bank[:, s, :], words[:, first : first + 2 * P - 1 : 2], identity[:]
-                        )
-                    banks.append((a, pair, bank))
+        def flip_direct(raw, h):
+            words = raw[:, HALF_COLS * h : HALF_COLS * (h + 1)].bitcast(F32)
+            bank = flipped_pool.tile([P, 4, P], F32, name="bank")
+            for g in range(HALF_PASSES):
+                for u in range(2):
+                    first = 2 * P * g + u
+                    nc.tensor.transpose(
+                        bank[:, 2 * g + u, :], words[:, first : first + 2 * P - 1 : 2], identity[:]
+                    )
+            return bank
 
-            grouped = []
-            for pair in range(PASSES // 2):
-                grouped.append(grouped_pool.tile([P, 2 * 4 * UNIT_COLS], BF16, name="grouped", align_bytes=64))
-            for n, (a, pair, bank) in enumerate(banks):
-                target = grouped[pair][:].bitcast(F32).rearrange(
-                    "p (g a c u) -> p g a c u", g=2, a=UNIT_TILES, u=2
-                )[:, :, a]
-                source = bank[:].rearrange("p (g u) c -> p g c u", u=2)
-                if (UNIT_BANKS * unit_number + n) % 3 == 2:
-                    nc.vector.tensor_copy(out=target, in_=source)
-                else:
-                    nc.scalar.copy(out=target, in_=source)
-
-            for pair in range(PASSES // 2):
-                two_passes = slice(2 * pair, 2 * pair + 2)
-                nc.vector.quantize_mx(
-                    out=codes[:, two_passes, :].rearrange("p g n -> p (g n)").bitcast(FP8X4),
-                    scales=scales[:, two_passes, :].rearrange("p g n -> p (g n)"),
-                    in_=grouped[pair][:],
-                )
+        def new_operand(name, tiles):
+            codes = quantised.tile([P, PASSES, tiles * P], U32, name=name + "_codes", align_bytes=64)
+            scales = quantised.tile([P, PASSES, tiles * P], U8, name=name + "_scales", align_bytes=64)
             return codes, scales
 
-        out_by_partition = out.rearrange("h (p i) d -> p h i d", p=P)
+        def new_grouped():
+            return grouped_pool.tile([P, 4 * P * 4], BF16, name="grouped", align_bytes=64)
 
-        def product(b, r, weight_unit, token_unit):
-            weight_codes, weight_scales = weight_unit
-            token_codes, token_scales = token_unit
-            groups = []
-            for a in range(UNIT_TILES):
-                cols = slice(P * a, P * (a + 1))
-                q = sums_pool.tile([P, UNIT_COLS], F32, name="q")
-                for g in range(PASSES):
-                    nc.tensor.matmul_mx(
-                        out=q[:],
-                        lhsT=token_codes[:, g, cols].bitcast(FP8X4),
-                        lhsT_scale=token_scales[:, g, cols],
-                        rhs=weight_codes[:, g, :].bitcast(FP8X4),
-                        rhs_scale=weight_scales[:, g, :],
-                        start=(g == 0),
-                        stop=(g == PASSES - 1),
-                    )
-                groups.append(q)
+        def empty(bank, target):
+            nc.scalar.copy(out=target, in_=bank[:].rearrange("p (g u) c -> p g c u", u=2))
 
-            pieces = [(a, h) for a in range(UNIT_TILES) for h in range(UNIT_TILES)]
-            squares = stats.tile([P, len(pieces), HEAD_DIM], F32, name="squares")
-            sum_squares = stats.tile([P, len(pieces)], F32, name="sum_squares")
-            for n, (a, h) in enumerate(pieces):
-                nc.scalar.activation(
-                    out=squares[:, n, :],
-                    in_=groups[a][:, HEAD_DIM * h : HEAD_DIM * (h + 1)],
-                    func=ACT.Square,
-                    accum_out=sum_squares[:, n : n + 1],
+        def weight_place(grouped, a):
+            return grouped[:].bitcast(F32).rearrange(
+                "p (g a c u) -> p g a c u", g=HALF_PASSES, a=UNIT_HEADS, u=2
+            )[:, :, a]
+
+        def token_place(grouped, h):
+            return grouped[:].bitcast(F32).rearrange(
+                "p (h g c u) -> p h g c u", h=HALVES, g=HALF_PASSES, u=2
+            )[:, h]
+
+        def quantise(grouped, operand, passes):
+            codes, scales = operand
+            nc.vector.quantize_mx(
+                out=codes[:, passes, :].rearrange("p g n -> p (g n)").bitcast(FP8X4),
+                scales=scales[:, passes, :].rearrange("p g n -> p (g n)"),
+                in_=grouped[:],
+            )
+
+        def half_passes(h):
+            return slice(HALF_PASSES * h, HALF_PASSES * (h + 1))
+
+        def multiply(b, i, heads=range(UNIT_HEADS), turning_bank=False):
+            weight_codes, weight_scales = weights[b]
+            token_codes, token_scales = tokens[i]
+            cols = slice(P * heads[0], P * (heads[-1] + 1))
+            if turning_bank:
+                bank = flipped_pool.tile([P, 4, P], F32, name="last_q", tag="bank")
+            else:
+                bank = sums_pool.tile([P, 4, P], F32, name="q")
+            q = bank[:, 0 : len(heads), :].rearrange("p h d -> p (h d)")
+            for g in range(PASSES):
+                nc.tensor.matmul_mx(
+                    out=q,
+                    lhsT=token_codes[:, g, :].bitcast(FP8X4),
+                    lhsT_scale=token_scales[:, g, :],
+                    rhs=weight_codes[:, g, cols].bitcast(FP8X4),
+                    rhs_scale=weight_scales[:, g, cols],
+                    start=(g == 0),
+                    stop=(g == PASSES - 1),
                 )
-            inv_rms = stats.tile([P, len(pieces)], F32, name="inv_rms")
+            for n, h in enumerate(heads):
+                sums[b, i, h] = bank[:, n, :]
+
+        def square(b, i, heads=range(UNIT_HEADS)):
+            if (b, i // 2) not in sum_squares:
+                sum_squares[b, i // 2] = stats.tile([P, 2, UNIT_HEADS], F32, name="sum_squares")
+                inverses[b, i // 2] = stats.tile([P, 2, UNIT_HEADS], F32, name="inv_rms")
+            squares = stats.tile([P, UNIT_HEADS, HEAD_DIM], F32, name="squares")
+            for h in heads:
+                nc.scalar.activation(
+                    out=squares[:, h, :],
+                    in_=sums[b, i, h],
+                    func=ACT.Square,
+                    accum_out=sum_squares[b, i // 2][:, i % 2, h : h + 1],
+                )
+
+        def invert(b, r, i=slice(0, 2), h=slice(0, UNIT_HEADS)):
             nc.scalar.activation(
-                out=inv_rms[:],
-                in_=sum_squares[:],
+                out=inverses[b, r][:, i, h],
+                in_=sum_squares[b, r][:, i, h],
                 func=ACT.Abs_reciprocal_sqrt,
                 scale=1.0 / HEAD_DIM,
                 bias=eps[:],
             )
-            result = results.tile([P, UNIT_TILES, UNIT_TILES, HEAD_DIM], F32, name="result")
-            for n, (a, h) in enumerate(pieces):
+
+        out_by_partition = out.rearrange("h (p i) d -> p h i d", p=P)
+
+        def scale(b, i, heads=range(UNIT_HEADS)):
+            r = i // 2
+            if (b, r) not in outcome:
+                outcome[b, r] = results.tile([P, UNIT_HEADS, 2, HEAD_DIM], F32, name="result")
+            for h in heads:
                 nc.vector.scalar_tensor_tensor(
-                    out=result[:, h, a, :],
-                    in0=groups[a][:, HEAD_DIM * h : HEAD_DIM * (h + 1)],
-                    scalar=inv_rms[:, n : n + 1],
+                    out=outcome[b, r][:, h, i % 2, :],
+                    in0=sums[b, i, h],
+                    scalar=inverses[b, r][:, i % 2, h : h + 1],
                     in1=gain[:],
                     op0=ALU.mult,
                     op1=ALU.mult,
                 )
+
+        def store(b, r, heads=range(UNIT_HEADS)):
             nc.sync.dma_start(
                 out=out_by_partition[
-                    :, UNIT_TILES * b : UNIT_TILES * (b + 1), UNIT_TILES * r : UNIT_TILES * (r + 1), :
+                    :, UNIT_HEADS * b + heads[0] : UNIT_HEADS * b + heads[-1] + 1, 2 * r : 2 * r + 2, :
                 ],
-                in_=result[:],
+                in_=outcome[b, r][:, heads[0] : heads[-1] + 1],
             )
 
-        keep_clock_up(IDLE_MATMULS_AT_START)
-        token_units = [quantise_unit(token_raw[0], "token0", 0)]
-        keep_clock_up(IDLE_MATMULS_A_UNIT)
-        weight_units = [quantise_unit(weight_raw[0], "weight0", 1)]
+        tokens, weights, sums, sum_squares, inverses, outcome = [], [], {}, {}, {}, {}
+
+        def turned(raw):
+            return [flip_direct(raw, h) for h in range(HALVES)]
+
+        def quantise_token(i, grouped):
+            operand = new_operand("token%d" % i, 1)
+            quantise(grouped, operand, slice(0, PASSES))
+            tokens.append(operand)
+
+        sorted_heads = []
+
+        def sort_next_head():
+            head = UNIT_HEADS + len(sorted_heads)
+            if head < HEADS:
+                sorted_heads.append([sort(weight_raw[head], h) for h in range(HALVES)])
+
+        keep_clock_up(6)
+        grouped_token = new_grouped()
+        banks = turned(token_raw[0])
+        for h in range(HALVES):
+            empty(banks[h], token_place(grouped_token, h))
+        weights.append(new_operand("weight0", UNIT_HEADS))
+        grouped = [new_grouped() for h in range(HALVES)]
+        for a in range(UNIT_HEADS):
+            banks = turned(weight_raw[a])
+            for h in range(HALVES):
+                empty(banks[h], weight_place(grouped[h], a))
+        quantise_token(0, grouped_token)
+        for h in range(HALVES):
+            quantise(grouped[h], weights[0], half_passes(h))
         spread_gain()
-        keep_clock_up(IDLE_MATMULS_A_UNIT)
-        token_units.append(quantise_unit(token_raw[1], "token1", 2))
-        product(0, 0, weight_units[0], token_units[0])
-        weight_units.append(quantise_unit(weight_raw[1], "weight1", 3))
-        product(0, 1, weight_units[0], token_units[1])
-        for b in range(1, WEIGHT_UNITS):
-            if b + 1 < WEIGHT_UNITS:
-                weight_units.append(quantise_unit(weight_raw[b + 1], "weight%d" % (b + 1), b + 3))
-            for r in range(TOKEN_UNITS):
-                product(b, r, weight_units[b], token_units[r])
+        for i in range(1, TOKEN_TILES):
+            grouped_token = new_grouped()
+            banks = turned(token_raw[i])
+            multiply(0, i - 1)
+            for h in range(HALVES):
+                empty(banks[h], token_place(grouped_token, h))
+            if i > 1:
+                sort_next_head()
+            if i == 3:
+                sort_next_head()
+            quantise_token(i, grouped_token)
+            square(0, i - 1)
+            if i == 3:
+                invert(0, 0)
+                scale(0, 0)
+                scale(0, 1)
+                store(0, 0)
+
+        for b in range(WEIGHT_UNITS):
+            more = b + 1 < WEIGHT_UNITS
+            if more:
+                weights.append(new_operand("weight%d" % (b + 1), UNIT_HEADS))
+                banks = [
+                    [flip(sorted_heads[UNIT_HEADS * b + a][h]) for a in range(UNIT_HEADS)] for h in range(HALVES)
+                ]
+                grouped = [new_grouped() for h in range(HALVES)]
+            if b > 0:
+                square(b - 1, 3)
+                if b > 1:
+                    scale(b - 1, 0)
+                    scale(b - 1, 1)
+                    store(b - 1, 0)
+            if more:
+                empty(banks[0][0], weight_place(grouped[0], 0))
+            if b > 0:
+                invert(b - 1, 1)
+            sort_next_head()
+            if b > 0:
+                scale(b - 1, 2)
+                scale(b - 1, 3)
+                store(b - 1, 1)
+            if more:
+                empty(banks[0][1], weight_place(grouped[0], 1))
+                quantise(grouped[0], weights[b + 1], half_passes(0))
+                empty(banks[1][0], weight_place(grouped[1], 0))
+                empty(banks[1][1], weight_place(grouped[1], 1))
+            sort_next_head()
+            if more:
+                quantise(grouped[1], weights[b + 1], half_passes(1))
+            if b == 0:
+                multiply(0, 3)
+            elif more:
+                for i in range(TOKEN_TILES):
+                    multiply(b, i)
+                    if i < 3:
+                        square(b, i)
+                invert(b, 0)
+        b = WEIGHT_UNITS - 1
+        multiply(b, 0, turning_bank=True)
+        square(b, 0)
+        multiply(b, 1, turning_bank=True)
+        square(b, 1)
+        invert(b, 0)
+        scale(b, 0)
+        scale(b, 1)
+        store(b, 0)
+        multiply(b, 2, turning_bank=True)
+        square(b, 2)
+        multiply(b, 3, [0], turning_bank=True)
+        square(b, 3, [0])
+        invert(b, 1, h=slice(0, 1))
+        scale(b, 2, [0])
+        scale(b, 3, [0])
+        store(b, 1, [0])
+        multiply(b, 3, [1])
+        square(b, 3, [1])
+        invert(b, 1, h=slice(1, 2))
+        scale(b, 2, [1])
+        scale(b, 3, [1])
+        store(b, 1, [1])

@@ -178,21 +178,22 @@ def tile_combcrossattention_pa_kernel(tc, hidden_states, Wq, q_norm_w, out):
 
         def square(b, i, heads=range(UNIT_HEADS)):
             if (b, i // 2) not in sum_squares:
-                sum_squares[b, i // 2] = stats.tile([P, 2, UNIT_HEADS], F32, name="sum_squares")
-                inverses[b, i // 2] = stats.tile([P, 2, UNIT_HEADS], F32, name="inv_rms")
+                sum_squares[b, i // 2] = stats.tile([P, 2 * UNIT_HEADS], F32, name="sum_squares")
+                inverses[b, i // 2] = stats.tile([P, 2 * UNIT_HEADS], F32, name="inv_rms")
             squares = stats.tile([P, UNIT_HEADS, HEAD_DIM], F32, name="squares")
             for h in heads:
+                n = UNIT_HEADS * (i % 2) + h
                 nc.scalar.activation(
                     out=squares[:, h, :],
                     in_=sums[b, i, h],
                     func=ACT.Square,
-                    accum_out=sum_squares[b, i // 2][:, i % 2, h : h + 1],
+                    accum_out=sum_squares[b, i // 2][:, n : n + 1],
                 )
 
-        def invert(b, r, i=slice(0, 2), h=slice(0, UNIT_HEADS)):
+        def invert(b, r, first=0, end=2 * UNIT_HEADS):
             nc.scalar.activation(
-                out=inverses[b, r][:, i, h],
-                in_=sum_squares[b, r][:, i, h],
+                out=inverses[b, r][:, first:end],
+                in_=sum_squares[b, r][:, first:end],
                 func=ACT.Abs_reciprocal_sqrt,
                 scale=1.0 / HEAD_DIM,
                 bias=eps[:],
@@ -205,10 +206,11 @@ def tile_combcrossattention_pa_kernel(tc, hidden_states, Wq, q_norm_w, out):
             if (b, r) not in outcome:
                 outcome[b, r] = results.tile([P, UNIT_HEADS, 2, HEAD_DIM], F32, name="result")
             for h in heads:
+                n = UNIT_HEADS * (i % 2) + h
                 nc.vector.scalar_tensor_tensor(
                     out=outcome[b, r][:, h, i % 2, :],
                     in0=sums[b, i, h],
-                    scalar=inverses[b, r][:, i % 2, h : h + 1],
+                    scalar=inverses[b, r][:, n : n + 1],
                     in1=gain[:],
                     op0=ALU.mult,
                     op1=ALU.mult,
@@ -242,21 +244,24 @@ def tile_combcrossattention_pa_kernel(tc, hidden_states, Wq, q_norm_w, out):
         keep_clock_up(6)
         grouped_token = new_grouped()
         banks = turned(token_raw[0])
+        keep_clock_up(2)
         for h in range(HALVES):
             empty(banks[h], token_place(grouped_token, h))
         weights.append(new_operand("weight0", UNIT_HEADS))
         grouped = [new_grouped() for h in range(HALVES)]
         for a in range(UNIT_HEADS):
             banks = turned(weight_raw[a])
+            keep_clock_up(1)
             for h in range(HALVES):
                 empty(banks[h], weight_place(grouped[h], a))
         quantise_token(0, grouped_token)
         for h in range(HALVES):
             quantise(grouped[h], weights[0], half_passes(h))
-        spread_gain()
         for i in range(1, TOKEN_TILES):
             grouped_token = new_grouped()
             banks = turned(token_raw[i])
+            if i == 2:
+                spread_gain()
             multiply(0, i - 1)
             for h in range(HALVES):
                 empty(banks[h], token_place(grouped_token, h))
@@ -324,13 +329,12 @@ def tile_combcrossattention_pa_kernel(tc, hidden_states, Wq, q_norm_w, out):
         square(b, 2)
         multiply(b, 3, [0], turning_bank=True)
         square(b, 3, [0])
-        invert(b, 1, h=slice(0, 1))
-        scale(b, 2, [0])
+        invert(b, 1, end=3)
+        scale(b, 2)
         scale(b, 3, [0])
         store(b, 1, [0])
         multiply(b, 3, [1])
         square(b, 3, [1])
-        invert(b, 1, h=slice(1, 2))
-        scale(b, 2, [1])
+        invert(b, 1, first=3)
         scale(b, 3, [1])
         store(b, 1, [1])

@@ -57,14 +57,17 @@ def tile_combcrossattention_pa_kernel(tc, hidden_states, Wq, q_norm_w, out):
                 nc.sync.dma_start(out=raw[:, cols], in_=tokens_by_partition[:, i, cols])
             token_raw.append(raw)
 
-        def load_weights(head):
+        def load_weights(head, pieces=1):
             raw = raw_pool.tile([P, EMBED], BF16, name="weight_raw%d" % head)
-            nc.sync.dma_start(out=raw[:], in_=Wq[P * head : P * (head + 1), :])
+            width = EMBED // pieces
+            for n in range(pieces):
+                cols = slice(width * n, width * (n + 1))
+                nc.sync.dma_start(out=raw[:, cols], in_=Wq[P * head : P * (head + 1), cols])
             weight_raw.append(raw)
 
         load_tokens(0, 2)
-        load_weights(0)
-        load_weights(1)
+        load_weights(0, 1)
+        load_weights(1, 1)
         for i in range(1, TOKEN_TILES):
             load_tokens(i, 1)
         for head in range(2, HEADS):
@@ -96,12 +99,16 @@ def tile_combcrossattention_pa_kernel(tc, hidden_states, Wq, q_norm_w, out):
             nc.tensor.matmul(out=bank[:, 0, :], lhsT=ones[:], rhs=gain_row[:], start=True, stop=True)
             nc.vector.tensor_copy(out=gain[:], in_=bank[:, 0, :])
 
-        def sort(raw, h):
+        def sort(raw, h, engine):
             words = sorted_pool.tile([P, 2, HALF_WORDS // 2], F32, name="words")
-            nc.vector.tensor_copy(
-                out=words[:],
-                in_=raw[:, HALF_COLS * h : HALF_COLS * (h + 1)].bitcast(F32).rearrange("p (w u) -> p u w", u=2),
-            )
+            source = raw[:, HALF_COLS * h : HALF_COLS * (h + 1)].bitcast(F32).rearrange("p (w u) -> p u w", u=2)
+            if engine == "vector":
+                nc.vector.tensor_copy(out=words[:], in_=source)
+            else:
+                for g in range(HALF_PASSES):
+                    nc.gpsimd.tensor_copy(
+                        out=words[:, :, P * g : P * (g + 1)], in_=source[:, :, P * g : P * (g + 1)]
+                    )
             return words
 
         def flip(words):
@@ -130,8 +137,12 @@ def tile_combcrossattention_pa_kernel(tc, hidden_states, Wq, q_norm_w, out):
         def new_grouped():
             return grouped_pool.tile([P, 4 * P * 4], BF16, name="grouped", align_bytes=64)
 
-        def empty(bank, target):
-            nc.scalar.copy(out=target, in_=bank[:].rearrange("p (g u) c -> p g c u", u=2))
+        def empty(bank, target, engine="scalar"):
+            source = bank[:].rearrange("p (g u) c -> p g c u", u=2)
+            if engine == "vector":
+                nc.vector.tensor_copy(out=target, in_=source)
+            else:
+                nc.scalar.copy(out=target, in_=source)
 
         def weight_place(grouped, a):
             return grouped[:].bitcast(F32).rearrange(
@@ -236,46 +247,70 @@ def tile_combcrossattention_pa_kernel(tc, hidden_states, Wq, q_norm_w, out):
 
         sorted_heads = []
 
-        def sort_next_head():
+        def sort_next_head(engine="vector"):
             head = UNIT_HEADS + len(sorted_heads)
             if head < HEADS:
-                sorted_heads.append([sort(weight_raw[head], h) for h in range(HALVES)])
+                sorted_heads.append([sort(weight_raw[head], h, engine) for h in range(HALVES)])
+
+        banks, words = {}, {}
+        raws = {"T0": token_raw[0], "T1": token_raw[1], "T2": token_raw[2], "T3": token_raw[3], "W0": weight_raw[0], "W1": weight_raw[1]}
+        tg = {}
+        grouped = [new_grouped() for h in range(HALVES)]
+        weights.append(new_operand("weight0", UNIT_HEADS))
+
+        def fl(x):
+            if x in words:
+                banks[x] = [flip(words[x][h]) for h in range(HALVES)]
+            else:
+                banks[x] = turned(raws[x])
+
+        def so(x, engine):
+            words[x] = [sort(raws[x], h, engine) for h in range(HALVES)]
+
+        def em(x):
+            if x[0] == "T":
+                tg[x] = new_grouped()
+            for h in range(HALVES):
+                empty(banks[x][h], token_place(tg[x], h) if x[0] == "T" else weight_place(grouped[h], int(x[1])))
+
+        def qt(i):
+            quantise_token(i, tg["T%d" % i])
+
+        def qw(h):
+            quantise(grouped[h], weights[0], half_passes(h))
 
         keep_clock_up(6)
-        grouped_token = new_grouped()
-        banks = turned(token_raw[0])
+        fl("T0")
         keep_clock_up(2)
-        for h in range(HALVES):
-            empty(banks[h], token_place(grouped_token, h))
-        weights.append(new_operand("weight0", UNIT_HEADS))
-        grouped = [new_grouped() for h in range(HALVES)]
-        for a in range(UNIT_HEADS):
-            banks = turned(weight_raw[a])
-            keep_clock_up(1)
-            for h in range(HALVES):
-                empty(banks[h], weight_place(grouped[h], a))
-        quantise_token(0, grouped_token)
-        for h in range(HALVES):
-            quantise(grouped[h], weights[0], half_passes(h))
-        for i in range(1, TOKEN_TILES):
-            grouped_token = new_grouped()
-            banks = turned(token_raw[i])
-            if i == 2:
-                spread_gain()
-            multiply(0, i - 1)
-            for h in range(HALVES):
-                empty(banks[h], token_place(grouped_token, h))
-            if i > 1:
-                sort_next_head()
-            if i == 3:
-                sort_next_head()
-            quantise_token(i, grouped_token)
-            square(0, i - 1)
-            if i == 3:
-                invert(0, 0)
-                scale(0, 0)
-                scale(0, 1)
-                store(0, 0)
+        em("T0")
+        fl("W0")
+        em("W0")
+        qt(0)
+        fl("W1")
+        em("W1")
+        qw(0)
+        qw(1)
+        fl("T1")
+        em("T1")
+        qt(1)
+        fl("T2")
+        spread_gain()
+        multiply(0, 0)
+        multiply(0, 1)
+        em("T2")
+        square(0, 0)
+        square(0, 1)
+        sort_next_head()
+        qt(2)
+        fl("T3")
+        em("T3")
+        sort_next_head()
+        sort_next_head()
+        qt(3)
+        invert(0, 0)
+        scale(0, 0)
+        scale(0, 1)
+        store(0, 0)
 
         for b in range(WEIGHT_UNITS):
             more = b + 1 < WEIGHT_UNITS
@@ -295,7 +330,7 @@ def tile_combcrossattention_pa_kernel(tc, hidden_states, Wq, q_norm_w, out):
                 empty(banks[0][0], weight_place(grouped[0], 0))
             if b > 0:
                 invert(b - 1, 1)
-            sort_next_head()
+            sort_next_head("vector")
             if b > 0:
                 scale(b - 1, 2)
                 scale(b - 1, 3)
@@ -304,11 +339,13 @@ def tile_combcrossattention_pa_kernel(tc, hidden_states, Wq, q_norm_w, out):
                 empty(banks[0][1], weight_place(grouped[0], 1))
                 quantise(grouped[0], weights[b + 1], half_passes(0))
                 empty(banks[1][0], weight_place(grouped[1], 0))
-                empty(banks[1][1], weight_place(grouped[1], 1))
-            sort_next_head()
+                empty(banks[1][1], weight_place(grouped[1], 1), "vector" if b % 3 == 2 else "scalar")
+            sort_next_head("vector")
             if more:
                 quantise(grouped[1], weights[b + 1], half_passes(1))
             if b == 0:
+                multiply(0, 2)
+                square(0, 2)
                 multiply(0, 3)
             elif more:
                 for i in range(TOKEN_TILES):

@@ -18,7 +18,9 @@ PASSES = EMBED // K_PASS
 HALVES = 2
 HALF_PASSES = PASSES // HALVES
 HALF_COLS = EMBED // HALVES
-HALF_WORDS = HALF_COLS // 2
+PASS_WORDS = 2 * P
+RUN = 8
+SORTED_PASSES = 4
 
 TOKEN_TILES = TOKENS // P
 UNIT_HEADS = 2
@@ -99,34 +101,31 @@ def tile_combcrossattention_pa_kernel(tc, hidden_states, Wq, q_norm_w, out):
             nc.tensor.matmul(out=bank[:, 0, :], lhsT=ones[:], rhs=gain_row[:], start=True, stop=True)
             nc.vector.tensor_copy(out=gain[:], in_=bank[:, 0, :])
 
-        def sort(raw, h, engine):
-            words = sorted_pool.tile([P, 2, HALF_WORDS // 2], F32, name="words")
-            source = raw[:, HALF_COLS * h : HALF_COLS * (h + 1)].bitcast(F32).rearrange("p (w u) -> p u w", u=2)
-            if engine == "vector":
-                nc.vector.tensor_copy(out=words[:], in_=source)
-            else:
-                for g in range(HALF_PASSES):
-                    nc.gpsimd.tensor_copy(
-                        out=words[:, :, P * g : P * (g + 1)], in_=source[:, :, P * g : P * (g + 1)]
-                    )
-            return words
+        def sort(raw, first, end):
+            end = min(end, SORTED_PASSES)
+            if first >= end:
+                return None
+            n = end - first
+            words = sorted_pool.tile([P, 2, n * P], F32, name="words%d" % n)
+            source = raw[:, K_PASS * first : K_PASS * end].bitcast(F32)
+            nc.vector.tensor_copy(
+                out=words[:].rearrange("p u (j i) -> p u j i", i=RUN),
+                in_=source.rearrange("p (j u i) -> p u j i", u=2, i=RUN),
+            )
+            return words, first
 
-        def flip(words):
+        def flip(raw, pieces, h):
             bank = flipped_pool.tile([P, 4, P], F32, name="bank")
-            for g in range(HALF_PASSES):
+            for n in range(HALF_PASSES):
+                g = HALF_PASSES * h + n
                 for u in range(2):
-                    nc.tensor.transpose(bank[:, 2 * g + u, :], words[:, u, P * g : P * (g + 1)], identity[:])
-            return bank
-
-        def flip_direct(raw, h):
-            words = raw[:, HALF_COLS * h : HALF_COLS * (h + 1)].bitcast(F32)
-            bank = flipped_pool.tile([P, 4, P], F32, name="bank")
-            for g in range(HALF_PASSES):
-                for u in range(2):
-                    first = 2 * P * g + u
-                    nc.tensor.transpose(
-                        bank[:, 2 * g + u, :], words[:, first : first + 2 * P - 1 : 2], identity[:]
-                    )
+                    if g < SORTED_PASSES:
+                        words, first = [x for x in pieces if x is not None and x[1] <= g][-1]
+                        source = words[:, u, P * (g - first) : P * (g - first + 1)]
+                    else:
+                        start = PASS_WORDS * g + u
+                        source = raw[:].bitcast(F32)[:, start : start + PASS_WORDS - 1 : 2]
+                    nc.tensor.transpose(bank[:, 2 * n + u, :], source, identity[:])
             return bank
 
         def new_operand(name, tiles):
@@ -237,9 +236,6 @@ def tile_combcrossattention_pa_kernel(tc, hidden_states, Wq, q_norm_w, out):
 
         tokens, weights, sums, sum_squares, inverses, outcome = [], [], {}, {}, {}, {}
 
-        def turned(raw):
-            return [flip_direct(raw, h) for h in range(HALVES)]
-
         def quantise_token(i, grouped):
             operand = new_operand("token%d" % i, 1)
             quantise(grouped, operand, slice(0, PASSES))
@@ -247,10 +243,10 @@ def tile_combcrossattention_pa_kernel(tc, hidden_states, Wq, q_norm_w, out):
 
         sorted_heads = []
 
-        def sort_next_head(engine="vector"):
+        def sort_next_head():
             head = UNIT_HEADS + len(sorted_heads)
             if head < HEADS:
-                sorted_heads.append([sort(weight_raw[head], h, engine) for h in range(HALVES)])
+                sorted_heads.append([sort(weight_raw[head], HALF_PASSES * h, HALF_PASSES * (h + 1)) for h in range(HALVES)])
 
         banks, words = {}, {}
         raws = {"T0": token_raw[0], "T1": token_raw[1], "T2": token_raw[2], "T3": token_raw[3], "W0": weight_raw[0], "W1": weight_raw[1]}
@@ -259,13 +255,10 @@ def tile_combcrossattention_pa_kernel(tc, hidden_states, Wq, q_norm_w, out):
         weights.append(new_operand("weight0", UNIT_HEADS))
 
         def fl(x):
-            if x in words:
-                banks[x] = [flip(words[x][h]) for h in range(HALVES)]
-            else:
-                banks[x] = turned(raws[x])
+            banks[x] = [flip(raws[x], words[x], h) for h in range(HALVES)]
 
-        def so(x, engine):
-            words[x] = [sort(raws[x], h, engine) for h in range(HALVES)]
+        def so(x):
+            words[x] = [sort(raws[x], HALF_PASSES * h, HALF_PASSES * (h + 1)) for h in range(HALVES)]
 
         def em(x):
             if x[0] == "T":
@@ -280,33 +273,41 @@ def tile_combcrossattention_pa_kernel(tc, hidden_states, Wq, q_norm_w, out):
             quantise(grouped[h], weights[0], half_passes(h))
 
         keep_clock_up(6)
+        so("T0")
         fl("T0")
         keep_clock_up(2)
         em("T0")
+        so("W0")
         fl("W0")
         em("W0")
         qt(0)
+        so("W1")
         fl("W1")
         em("W1")
-        qw(0)
-        qw(1)
+        so("T1")
+
         fl("T1")
         em("T1")
-        qt(1)
+        so("T2")
         fl("T2")
-        spread_gain()
+        qw(0)
+        qw(1)
         multiply(0, 0)
-        multiply(0, 1)
         em("T2")
-        square(0, 0)
-        square(0, 1)
-        sort_next_head()
-        qt(2)
+        so("T3")
         fl("T3")
+        qt(1)
+        square(0, 0)
+        multiply(0, 1)
         em("T3")
         sort_next_head()
+        spread_gain()
+        qt(2)
+        square(0, 1)
         sort_next_head()
         qt(3)
+        sort_next_head()
+
         invert(0, 0)
         scale(0, 0)
         scale(0, 1)
@@ -317,7 +318,7 @@ def tile_combcrossattention_pa_kernel(tc, hidden_states, Wq, q_norm_w, out):
             if more:
                 weights.append(new_operand("weight%d" % (b + 1), UNIT_HEADS))
                 banks = [
-                    [flip(sorted_heads[UNIT_HEADS * b + a][h]) for a in range(UNIT_HEADS)] for h in range(HALVES)
+                    [flip(weight_raw[UNIT_HEADS * (b + 1) + a], sorted_heads[UNIT_HEADS * b + a], h) for a in range(UNIT_HEADS)] for h in range(HALVES)
                 ]
                 grouped = [new_grouped() for h in range(HALVES)]
             if b > 0:
@@ -330,7 +331,7 @@ def tile_combcrossattention_pa_kernel(tc, hidden_states, Wq, q_norm_w, out):
                 empty(banks[0][0], weight_place(grouped[0], 0))
             if b > 0:
                 invert(b - 1, 1)
-            sort_next_head("vector")
+            sort_next_head()
             if b > 0:
                 scale(b - 1, 2)
                 scale(b - 1, 3)
@@ -339,8 +340,8 @@ def tile_combcrossattention_pa_kernel(tc, hidden_states, Wq, q_norm_w, out):
                 empty(banks[0][1], weight_place(grouped[0], 1))
                 quantise(grouped[0], weights[b + 1], half_passes(0))
                 empty(banks[1][0], weight_place(grouped[1], 0))
-                empty(banks[1][1], weight_place(grouped[1], 1), "vector" if b % 3 == 2 else "scalar")
-            sort_next_head("vector")
+                empty(banks[1][1], weight_place(grouped[1], 1), "vector" if False else "scalar")
+            sort_next_head()
             if more:
                 quantise(grouped[1], weights[b + 1], half_passes(1))
             if b == 0:

@@ -279,6 +279,7 @@ def tile_combcrossattention_pa_kernel(tc, hidden_states, Wq, q_norm_w, out):
         em("T0")
         so("W0")
         fl("W0")
+        keep_clock_up(2)
         em("W0")
         qt(0)
         so("W1")
@@ -287,11 +288,13 @@ def tile_combcrossattention_pa_kernel(tc, hidden_states, Wq, q_norm_w, out):
         so("T1")
 
         fl("T1")
+        keep_clock_up(1)
         em("T1")
         so("T2")
         fl("T2")
         qw(0)
         qw(1)
+        spread_gain()
         multiply(0, 0)
         em("T2")
         so("T3")
@@ -301,7 +304,6 @@ def tile_combcrossattention_pa_kernel(tc, hidden_states, Wq, q_norm_w, out):
         multiply(0, 1)
         em("T3")
         sort_next_head()
-        spread_gain()
         qt(2)
         square(0, 1)
         sort_next_head()

@@ -272,7 +272,7 @@ def tile_combcrossattention_pa_kernel(tc, hidden_states, Wq, q_norm_w, out):
         def qw(h):
             quantise(grouped[h], weights[0], half_passes(h))
 
-        keep_clock_up(6)
+        keep_clock_up(4)
         so("T0")
         fl("T0")
         keep_clock_up(2)
@@ -281,8 +281,8 @@ def tile_combcrossattention_pa_kernel(tc, hidden_states, Wq, q_norm_w, out):
         fl("W0")
         keep_clock_up(2)
         em("W0")
-        qt(0)
         so("W1")
+        qt(0)
         fl("W1")
         em("W1")
         so("T1")

@@ -19,8 +19,6 @@ HALVES = 2
 HALF_PASSES = PASSES // HALVES
 HALF_COLS = EMBED // HALVES
 PASS_WORDS = 2 * P
-RUN = 8
-SORTED_PASSES = 4
 
 TOKEN_TILES = TOKENS // P
 UNIT_HEADS = 2
@@ -42,7 +40,7 @@ def tile_combcrossattention_pa_kernel(tc, hidden_states, Wq, q_norm_w, out):
         tc.tile_pool(name="quantised", bufs=1) as quantised,
         tc.tile_pool(name="grouped", bufs=4) as grouped_pool,
         tc.tile_pool(name="stats", bufs=6) as stats,
-        tc.tile_pool(name="results", bufs=8) as results,
+        tc.tile_pool(name="results", bufs=16) as results,
         tc.psum_pool(name="flipped", bufs=4) as flipped_pool,
         tc.psum_pool(name="sums", bufs=4) as sums_pool,
         tc.manual_schedule(),
@@ -102,15 +100,12 @@ def tile_combcrossattention_pa_kernel(tc, hidden_states, Wq, q_norm_w, out):
             nc.vector.tensor_copy(out=gain[:], in_=bank[:, 0, :])
 
         def sort(raw, first, end):
-            end = min(end, SORTED_PASSES)
-            if first >= end:
-                return None
             n = end - first
             words = sorted_pool.tile([P, 2, n * P], F32, name="words%d" % n)
             source = raw[:, K_PASS * first : K_PASS * end].bitcast(F32)
             nc.vector.tensor_copy(
-                out=words[:].rearrange("p u (j i) -> p u j i", i=RUN),
-                in_=source.rearrange("p (j u i) -> p u j i", u=2, i=RUN),
+                out=words[:],
+                in_=source.rearrange("p (i u) -> p u i", u=2),
             )
             return words, first
 
@@ -119,8 +114,8 @@ def tile_combcrossattention_pa_kernel(tc, hidden_states, Wq, q_norm_w, out):
             for n in range(HALF_PASSES):
                 g = HALF_PASSES * h + n
                 for u in range(2):
-                    if g < SORTED_PASSES:
-                        words, first = [x for x in pieces if x is not None and x[1] <= g][-1]
+                    if pieces is not None:
+                        words, first = [x for x in pieces if x[1] <= g][-1]
                         source = words[:, u, P * (g - first) : P * (g - first + 1)]
                     else:
                         start = PASS_WORDS * g + u
@@ -245,7 +240,9 @@ def tile_combcrossattention_pa_kernel(tc, hidden_states, Wq, q_norm_w, out):
 
         def sort_next_head():
             head = UNIT_HEADS + len(sorted_heads)
-            if head < HEADS:
+            if head < HEADS and head == 3:
+                sorted_heads.append(None)
+            elif head < HEADS:
                 sorted_heads.append([sort(weight_raw[head], HALF_PASSES * h, HALF_PASSES * (h + 1)) for h in range(HALVES)])
 
         banks, words = {}, {}
@@ -255,16 +252,20 @@ def tile_combcrossattention_pa_kernel(tc, hidden_states, Wq, q_norm_w, out):
         weights.append(new_operand("weight0", UNIT_HEADS))
 
         def fl(x):
-            banks[x] = [flip(raws[x], words[x], h) for h in range(HALVES)]
+            banks[x] = [flip(raws[x], words.get(x), h) for h in range(HALVES)]
 
         def so(x):
             words[x] = [sort(raws[x], HALF_PASSES * h, HALF_PASSES * (h + 1)) for h in range(HALVES)]
 
-        def em(x):
+        def em(x, by_vector=()):
             if x[0] == "T":
                 tg[x] = new_grouped()
             for h in range(HALVES):
-                empty(banks[x][h], token_place(tg[x], h) if x[0] == "T" else weight_place(grouped[h], int(x[1])))
+                empty(
+                    banks[x][h],
+                    token_place(tg[x], h) if x[0] == "T" else weight_place(grouped[h], int(x[1])),
+                    "vector" if h in by_vector else "scalar",
+                )
 
         def qt(i):
             quantise_token(i, tg["T%d" % i])
@@ -273,31 +274,25 @@ def tile_combcrossattention_pa_kernel(tc, hidden_states, Wq, q_norm_w, out):
             quantise(grouped[h], weights[0], half_passes(h))
 
         keep_clock_up(4)
-        so("T0")
         fl("T0")
         keep_clock_up(2)
         em("T0")
-        so("W0")
         fl("W0")
-        keep_clock_up(2)
+        keep_clock_up(1)
         em("W0")
-        so("W1")
         qt(0)
         fl("W1")
         em("W1")
-        so("T1")
 
         fl("T1")
         keep_clock_up(1)
         em("T1")
-        so("T2")
         fl("T2")
         qw(0)
         qw(1)
         spread_gain()
         multiply(0, 0)
         em("T2")
-        so("T3")
         fl("T3")
         qt(1)
         square(0, 0)
@@ -308,7 +303,6 @@ def tile_combcrossattention_pa_kernel(tc, hidden_states, Wq, q_norm_w, out):
         square(0, 1)
         sort_next_head()
         qt(3)
-        sort_next_head()
 
         invert(0, 0)
         scale(0, 0)
@@ -323,29 +317,45 @@ def tile_combcrossattention_pa_kernel(tc, hidden_states, Wq, q_norm_w, out):
                     [flip(weight_raw[UNIT_HEADS * (b + 1) + a], sorted_heads[UNIT_HEADS * b + a], h) for a in range(UNIT_HEADS)] for h in range(HALVES)
                 ]
                 grouped = [new_grouped() for h in range(HALVES)]
-            if b > 0:
+            if b == WEIGHT_UNITS - 2:
                 square(b - 1, 3)
-                if b > 1:
-                    scale(b - 1, 0)
-                    scale(b - 1, 1)
-                    store(b - 1, 0)
-            if more:
+                scale(b - 1, 0)
+                scale(b - 1, 1)
+                store(b - 1, 0)
                 empty(banks[0][0], weight_place(grouped[0], 0))
-            if b > 0:
+                empty(banks[0][1], weight_place(grouped[0], 1), "vector")
                 invert(b - 1, 1)
-            sort_next_head()
-            if b > 0:
                 scale(b - 1, 2)
                 scale(b - 1, 3)
                 store(b - 1, 1)
-            if more:
-                empty(banks[0][1], weight_place(grouped[0], 1))
                 quantise(grouped[0], weights[b + 1], half_passes(0))
                 empty(banks[1][0], weight_place(grouped[1], 0))
-                empty(banks[1][1], weight_place(grouped[1], 1), "vector" if False else "scalar")
-            sort_next_head()
-            if more:
+                empty(banks[1][1], weight_place(grouped[1], 1))
                 quantise(grouped[1], weights[b + 1], half_passes(1))
+            else:
+                if b > 0:
+                    square(b - 1, 3)
+                    if b > 1:
+                        scale(b - 1, 0)
+                        scale(b - 1, 1)
+                        store(b - 1, 0)
+                if more:
+                    empty(banks[0][0], weight_place(grouped[0], 0))
+                if b > 0:
+                    invert(b - 1, 1)
+                sort_next_head()
+                if b > 0:
+                    scale(b - 1, 2)
+                    scale(b - 1, 3)
+                    store(b - 1, 1)
+                if more:
+                    empty(banks[0][1], weight_place(grouped[0], 1))
+                    quantise(grouped[0], weights[b + 1], half_passes(0))
+                    empty(banks[1][0], weight_place(grouped[1], 0))
+                    empty(banks[1][1], weight_place(grouped[1], 1))
+                sort_next_head()
+                if more:
+                    quantise(grouped[1], weights[b + 1], half_passes(1))
             if b == 0:
                 multiply(0, 2)
                 square(0, 2)

@@ -15,17 +15,26 @@ EPS = 1e-05
 
 K_PASS = 4 * P
 PASSES = EMBED // K_PASS
+PASS_WORDS = K_PASS // 2
 HALVES = 2
 HALF_PASSES = PASSES // HALVES
 HALF_COLS = EMBED // HALVES
-PASS_WORDS = 2 * P
 
 TOKEN_TILES = TOKENS // P
+PAIR_TILES = 2
 UNIT_HEADS = 2
 UNIT_COLS = UNIT_HEADS * P
 WEIGHT_UNITS = HEADS // UNIT_HEADS
+PAIR_PIECES = PAIR_TILES * UNIT_HEADS
 
+DIRECT_HEAD = 3
+
+IDLE_AT_START = 4
 IDLE_COLS = 512
+
+SORTED_BUFS = 10
+GROUPED_BUFS = 4
+RESULT_BUFS = WEIGHT_UNITS * TOKEN_TILES // PAIR_TILES
 
 FLOPS = 2 * TOKENS * EMBED * HEADS * HEAD_DIM
 
@@ -36,20 +45,20 @@ def tile_combcrossattention_pa_kernel(tc, hidden_states, Wq, q_norm_w, out):
     with (
         tc.tile_pool(name="consts", bufs=1) as consts,
         tc.tile_pool(name="raw", bufs=1) as raw_pool,
-        tc.tile_pool(name="sorted", bufs=10) as sorted_pool,
+        tc.tile_pool(name="sorted", bufs=SORTED_BUFS) as sorted_pool,
         tc.tile_pool(name="quantised", bufs=1) as quantised,
-        tc.tile_pool(name="grouped", bufs=4) as grouped_pool,
+        tc.tile_pool(name="grouped", bufs=GROUPED_BUFS) as grouped_pool,
         tc.tile_pool(name="stats", bufs=6) as stats,
-        tc.tile_pool(name="results", bufs=16) as results,
-        tc.psum_pool(name="flipped", bufs=4) as flipped_pool,
-        tc.psum_pool(name="sums", bufs=4) as sums_pool,
+        tc.tile_pool(name="results", bufs=RESULT_BUFS) as results,
+        tc.psum_pool(name="turned", bufs=4) as turned_pool,
+        tc.psum_pool(name="sums", bufs=TOKEN_TILES) as sums_pool,
         tc.manual_schedule(),
     ):
         tokens_by_partition = hidden_states.rearrange("(p i) k -> p i k", p=P)
         token_raw = []
         weight_raw = []
 
-        def load_tokens(i, pieces):
+        def load_tokens(i, pieces=1):
             raw = raw_pool.tile([P, EMBED], BF16, name="token_raw%d" % i)
             width = EMBED // pieces
             for n in range(pieces):
@@ -57,19 +66,16 @@ def tile_combcrossattention_pa_kernel(tc, hidden_states, Wq, q_norm_w, out):
                 nc.sync.dma_start(out=raw[:, cols], in_=tokens_by_partition[:, i, cols])
             token_raw.append(raw)
 
-        def load_weights(head, pieces=1):
+        def load_weights(head):
             raw = raw_pool.tile([P, EMBED], BF16, name="weight_raw%d" % head)
-            width = EMBED // pieces
-            for n in range(pieces):
-                cols = slice(width * n, width * (n + 1))
-                nc.sync.dma_start(out=raw[:, cols], in_=Wq[P * head : P * (head + 1), cols])
+            nc.sync.dma_start(out=raw[:], in_=Wq[P * head : P * (head + 1), :])
             weight_raw.append(raw)
 
-        load_tokens(0, 2)
-        load_weights(0, 1)
-        load_weights(1, 1)
+        load_tokens(0, pieces=HALVES)
+        load_weights(0)
+        load_weights(1)
         for i in range(1, TOKEN_TILES):
-            load_tokens(i, 1)
+            load_tokens(i)
         for head in range(2, HEADS):
             load_weights(head)
 
@@ -95,33 +101,33 @@ def tile_combcrossattention_pa_kernel(tc, hidden_states, Wq, q_norm_w, out):
                 nc.tensor.matmul(out=unread[:], lhsT=ones[:], rhs=idle_rhs[:], start=True, stop=True)
 
         def spread_gain():
-            bank = flipped_pool.tile([P, 4, P], F32, name="bank")
+            bank = turned_pool.tile([P, 4, P], F32, name="bank")
             nc.tensor.matmul(out=bank[:, 0, :], lhsT=ones[:], rhs=gain_row[:], start=True, stop=True)
             nc.vector.tensor_copy(out=gain[:], in_=bank[:, 0, :])
 
-        def sort(raw, first, end):
-            n = end - first
-            words = sorted_pool.tile([P, 2, n * P], F32, name="words%d" % n)
-            source = raw[:, K_PASS * first : K_PASS * end].bitcast(F32)
-            nc.vector.tensor_copy(
-                out=words[:],
-                in_=source.rearrange("p (i u) -> p u i", u=2),
-            )
-            return words, first
+        def sort(raw):
+            halves = []
+            for h in range(HALVES):
+                words = sorted_pool.tile([P, 2, HALF_COLS // 4], F32, name="words")
+                half = raw[:, HALF_COLS * h : HALF_COLS * (h + 1)].bitcast(F32)
+                nc.vector.tensor_copy(out=words[:], in_=half.rearrange("p (w u) -> p u w", u=2))
+                halves.append(words)
+            return halves
 
-        def flip(raw, pieces, h):
-            bank = flipped_pool.tile([P, 4, P], F32, name="bank")
+        def turn_half(raw, words, h):
+            bank = turned_pool.tile([P, 4, P], F32, name="bank")
             for n in range(HALF_PASSES):
-                g = HALF_PASSES * h + n
                 for u in range(2):
-                    if pieces is not None:
-                        words, first = [x for x in pieces if x[1] <= g][-1]
-                        source = words[:, u, P * (g - first) : P * (g - first + 1)]
+                    if words is None:
+                        first = PASS_WORDS * (HALF_PASSES * h + n) + u
+                        source = raw[:].bitcast(F32)[:, first : first + PASS_WORDS - 1 : 2]
                     else:
-                        start = PASS_WORDS * g + u
-                        source = raw[:].bitcast(F32)[:, start : start + PASS_WORDS - 1 : 2]
+                        source = words[h][:, u, P * n : P * (n + 1)]
                     nc.tensor.transpose(bank[:, 2 * n + u, :], source, identity[:])
             return bank
+
+        def turn(raw, words=None):
+            return [turn_half(raw, words, h) for h in range(HALVES)]
 
         def new_operand(name, tiles):
             codes = quantised.tile([P, PASSES, tiles * P], U32, name=name + "_codes", align_bytes=64)
@@ -131,42 +137,48 @@ def tile_combcrossattention_pa_kernel(tc, hidden_states, Wq, q_norm_w, out):
         def new_grouped():
             return grouped_pool.tile([P, 4 * P * 4], BF16, name="grouped", align_bytes=64)
 
-        def empty(bank, target, engine="scalar"):
-            source = bank[:].rearrange("p (g u) c -> p g c u", u=2)
-            if engine == "vector":
-                nc.vector.tensor_copy(out=target, in_=source)
-            else:
-                nc.scalar.copy(out=target, in_=source)
+        def empty(bank, target, copy=nc.scalar.copy):
+            copy(out=target, in_=bank[:].rearrange("p (g u) c -> p g c u", u=2))
 
         def weight_place(grouped, a):
             return grouped[:].bitcast(F32).rearrange(
                 "p (g a c u) -> p g a c u", g=HALF_PASSES, a=UNIT_HEADS, u=2
             )[:, :, a]
 
-        def token_place(grouped, h):
-            return grouped[:].bitcast(F32).rearrange(
+        def empty_token_banks(banks):
+            grouped = new_grouped()
+            places = grouped[:].bitcast(F32).rearrange(
                 "p (h g c u) -> p h g c u", h=HALVES, g=HALF_PASSES, u=2
-            )[:, h]
+            )
+            for h in range(HALVES):
+                empty(banks[h], places[:, h])
+            return grouped
 
-        def quantise(grouped, operand, passes):
+        def quantise(grouped, operand, first_pass, end_pass):
             codes, scales = operand
             nc.vector.quantize_mx(
-                out=codes[:, passes, :].rearrange("p g n -> p (g n)").bitcast(FP8X4),
-                scales=scales[:, passes, :].rearrange("p g n -> p (g n)"),
+                out=codes[:, first_pass:end_pass, :].rearrange("p g n -> p (g n)").bitcast(FP8X4),
+                scales=scales[:, first_pass:end_pass, :].rearrange("p g n -> p (g n)"),
                 in_=grouped[:],
             )
 
-        def half_passes(h):
-            return slice(HALF_PASSES * h, HALF_PASSES * (h + 1))
+        def quantise_tokens(i, grouped):
+            tokens.append(new_operand("token%d" % i, 1))
+            quantise(grouped, tokens[i], 0, PASSES)
 
-        def multiply(b, i, heads=range(UNIT_HEADS), turning_bank=False):
+        def quantise_weights(b, grouped, h):
+            quantise(grouped[h], weights[b], HALF_PASSES * h, HALF_PASSES * (h + 1))
+
+        sorted_heads = {}
+
+        def sort_head(head):
+            sorted_heads[head] = None if head == DIRECT_HEAD else sort(weight_raw[head])
+
+        def multiply(b, i, heads=range(UNIT_HEADS), pool=sums_pool, tag="q"):
             weight_codes, weight_scales = weights[b]
             token_codes, token_scales = tokens[i]
             cols = slice(P * heads[0], P * (heads[-1] + 1))
-            if turning_bank:
-                bank = flipped_pool.tile([P, 4, P], F32, name="last_q", tag="bank")
-            else:
-                bank = sums_pool.tile([P, 4, P], F32, name="q")
+            bank = pool.tile([P, 4, P], F32, name="q", tag=tag)
             q = bank[:, 0 : len(heads), :].rearrange("p h d -> p (h d)")
             for g in range(PASSES):
                 nc.tensor.matmul_mx(
@@ -181,210 +193,161 @@ def tile_combcrossattention_pa_kernel(tc, hidden_states, Wq, q_norm_w, out):
             for n, h in enumerate(heads):
                 sums[b, i, h] = bank[:, n, :]
 
+        def piece(i, h):
+            return UNIT_HEADS * (i % PAIR_TILES) + h
+
         def square(b, i, heads=range(UNIT_HEADS)):
-            if (b, i // 2) not in sum_squares:
-                sum_squares[b, i // 2] = stats.tile([P, 2 * UNIT_HEADS], F32, name="sum_squares")
-                inverses[b, i // 2] = stats.tile([P, 2 * UNIT_HEADS], F32, name="inv_rms")
+            pair = b, i // PAIR_TILES
+            if pair not in sum_squares:
+                sum_squares[pair] = stats.tile([P, PAIR_PIECES], F32, name="sum_squares")
+                inv_rms[pair] = stats.tile([P, PAIR_PIECES], F32, name="inv_rms")
+                outcome[pair] = results.tile([P, UNIT_HEADS, PAIR_TILES, HEAD_DIM], F32, name="result")
             squares = stats.tile([P, UNIT_HEADS, HEAD_DIM], F32, name="squares")
             for h in heads:
-                n = UNIT_HEADS * (i % 2) + h
+                n = piece(i, h)
                 nc.scalar.activation(
                     out=squares[:, h, :],
                     in_=sums[b, i, h],
                     func=ACT.Square,
-                    accum_out=sum_squares[b, i // 2][:, n : n + 1],
+                    accum_out=sum_squares[pair][:, n : n + 1],
                 )
 
-        def invert(b, r, first=0, end=2 * UNIT_HEADS):
+        def invert(b, r, first=0, end=PAIR_PIECES):
             nc.scalar.activation(
-                out=inverses[b, r][:, first:end],
+                out=inv_rms[b, r][:, first:end],
                 in_=sum_squares[b, r][:, first:end],
                 func=ACT.Abs_reciprocal_sqrt,
                 scale=1.0 / HEAD_DIM,
                 bias=eps[:],
             )
 
-        out_by_partition = out.rearrange("h (p i) d -> p h i d", p=P)
-
         def scale(b, i, heads=range(UNIT_HEADS)):
-            r = i // 2
-            if (b, r) not in outcome:
-                outcome[b, r] = results.tile([P, UNIT_HEADS, 2, HEAD_DIM], F32, name="result")
+            pair = b, i // PAIR_TILES
             for h in heads:
-                n = UNIT_HEADS * (i % 2) + h
+                n = piece(i, h)
                 nc.vector.scalar_tensor_tensor(
-                    out=outcome[b, r][:, h, i % 2, :],
+                    out=outcome[pair][:, h, i % PAIR_TILES, :],
                     in0=sums[b, i, h],
-                    scalar=inverses[b, r][:, n : n + 1],
+                    scalar=inv_rms[pair][:, n : n + 1],
                     in1=gain[:],
                     op0=ALU.mult,
                     op1=ALU.mult,
                 )
 
+        out_by_partition = out.rearrange("h (p i) d -> p h i d", p=P)
+
         def store(b, r, heads=range(UNIT_HEADS)):
             nc.sync.dma_start(
                 out=out_by_partition[
-                    :, UNIT_HEADS * b + heads[0] : UNIT_HEADS * b + heads[-1] + 1, 2 * r : 2 * r + 2, :
+                    :,
+                    UNIT_HEADS * b + heads[0] : UNIT_HEADS * b + heads[-1] + 1,
+                    PAIR_TILES * r : PAIR_TILES * (r + 1),
+                    :,
                 ],
                 in_=outcome[b, r][:, heads[0] : heads[-1] + 1],
             )
 
-        tokens, weights, sums, sum_squares, inverses, outcome = [], [], {}, {}, {}, {}
+        def scale_and_store_pair(b, r):
+            for i in range(PAIR_TILES * r, PAIR_TILES * (r + 1)):
+                scale(b, i)
+            store(b, r)
 
-        def quantise_token(i, grouped):
-            operand = new_operand("token%d" % i, 1)
-            quantise(grouped, operand, slice(0, PASSES))
-            tokens.append(operand)
+        tokens, weights = [], []
+        sums, sum_squares, inv_rms, outcome = {}, {}, {}, {}
 
-        sorted_heads = []
-
-        def sort_next_head():
-            head = UNIT_HEADS + len(sorted_heads)
-            if head < HEADS and head == 3:
-                sorted_heads.append(None)
-            elif head < HEADS:
-                sorted_heads.append([sort(weight_raw[head], HALF_PASSES * h, HALF_PASSES * (h + 1)) for h in range(HALVES)])
-
-        banks, words = {}, {}
-        raws = {"T0": token_raw[0], "T1": token_raw[1], "T2": token_raw[2], "T3": token_raw[3], "W0": weight_raw[0], "W1": weight_raw[1]}
-        tg = {}
-        grouped = [new_grouped() for h in range(HALVES)]
+        keep_clock_up(IDLE_AT_START)
         weights.append(new_operand("weight0", UNIT_HEADS))
-
-        def fl(x):
-            banks[x] = [flip(raws[x], words.get(x), h) for h in range(HALVES)]
-
-        def so(x):
-            words[x] = [sort(raws[x], HALF_PASSES * h, HALF_PASSES * (h + 1)) for h in range(HALVES)]
-
-        def em(x, by_vector=()):
-            if x[0] == "T":
-                tg[x] = new_grouped()
-            for h in range(HALVES):
-                empty(
-                    banks[x][h],
-                    token_place(tg[x], h) if x[0] == "T" else weight_place(grouped[h], int(x[1])),
-                    "vector" if h in by_vector else "scalar",
-                )
-
-        def qt(i):
-            quantise_token(i, tg["T%d" % i])
-
-        def qw(h):
-            quantise(grouped[h], weights[0], half_passes(h))
-
-        keep_clock_up(4)
-        fl("T0")
+        grouped = [new_grouped() for h in range(HALVES)]
+        banks = turn(token_raw[0], sort(token_raw[0]))
         keep_clock_up(2)
-        em("T0")
-        fl("W0")
+        grouped_tokens = [empty_token_banks(banks)]
+        banks = turn(weight_raw[0], sort(weight_raw[0]))
+        keep_clock_up(2)
+        for h in range(HALVES):
+            empty(banks[h], weight_place(grouped[h], 0))
+        words = sort(weight_raw[1])
+        quantise_tokens(0, grouped_tokens[0])
+        banks = turn(weight_raw[1], words)
         keep_clock_up(1)
-        em("W0")
-        qt(0)
-        fl("W1")
-        em("W1")
-
-        fl("T1")
+        for h in range(HALVES):
+            empty(banks[h], weight_place(grouped[h], 1))
+        banks = turn(token_raw[1])
         keep_clock_up(1)
-        em("T1")
-        fl("T2")
-        qw(0)
-        qw(1)
+        grouped_tokens.append(empty_token_banks(banks))
+        banks = turn(token_raw[2])
+        for h in range(HALVES):
+            quantise_weights(0, grouped, h)
         spread_gain()
         multiply(0, 0)
-        em("T2")
-        fl("T3")
-        qt(1)
+        grouped_tokens.append(empty_token_banks(banks))
+        banks = turn(token_raw[3])
+        quantise_tokens(1, grouped_tokens[1])
         square(0, 0)
         multiply(0, 1)
-        em("T3")
-        sort_next_head()
-        qt(2)
+        grouped_tokens.append(empty_token_banks(banks))
+        sort_head(2)
+        quantise_tokens(2, grouped_tokens[2])
         square(0, 1)
-        sort_next_head()
-        qt(3)
-
+        sort_head(3)
+        quantise_tokens(3, grouped_tokens[3])
         invert(0, 0)
-        scale(0, 0)
-        scale(0, 1)
-        store(0, 0)
+        scale_and_store_pair(0, 0)
 
-        for b in range(WEIGHT_UNITS):
-            more = b + 1 < WEIGHT_UNITS
-            if more:
-                weights.append(new_operand("weight%d" % (b + 1), UNIT_HEADS))
-                banks = [
-                    [flip(weight_raw[UNIT_HEADS * (b + 1) + a], sorted_heads[UNIT_HEADS * b + a], h) for a in range(UNIT_HEADS)] for h in range(HALVES)
-                ]
-                grouped = [new_grouped() for h in range(HALVES)]
-            if b == WEIGHT_UNITS - 2:
+        for b in range(WEIGHT_UNITS - 1):
+            heads_to_sort = range(UNIT_HEADS * (b + 2), min(UNIT_HEADS * (b + 3), HEADS))
+            weights.append(new_operand("weight%d" % (b + 1), UNIT_HEADS))
+            banks = [
+                [turn_half(weight_raw[head], sorted_heads[head], h) for head in (2 * b + 2, 2 * b + 3)]
+                for h in range(HALVES)
+            ]
+            grouped = [new_grouped() for h in range(HALVES)]
+            if b > 0:
                 square(b - 1, 3)
-                scale(b - 1, 0)
-                scale(b - 1, 1)
-                store(b - 1, 0)
-                empty(banks[0][0], weight_place(grouped[0], 0))
-                empty(banks[0][1], weight_place(grouped[0], 1), "vector")
+                if b > 1:
+                    scale_and_store_pair(b - 1, 0)
+            empty(banks[0][0], weight_place(grouped[0], 0))
+            if b > 0:
                 invert(b - 1, 1)
-                scale(b - 1, 2)
-                scale(b - 1, 3)
-                store(b - 1, 1)
-                quantise(grouped[0], weights[b + 1], half_passes(0))
-                empty(banks[1][0], weight_place(grouped[1], 0))
-                empty(banks[1][1], weight_place(grouped[1], 1))
-                quantise(grouped[1], weights[b + 1], half_passes(1))
+            if heads_to_sort:
+                sort_head(heads_to_sort[0])
+                empty(banks[0][1], weight_place(grouped[0], 1))
             else:
-                if b > 0:
-                    square(b - 1, 3)
-                    if b > 1:
-                        scale(b - 1, 0)
-                        scale(b - 1, 1)
-                        store(b - 1, 0)
-                if more:
-                    empty(banks[0][0], weight_place(grouped[0], 0))
-                if b > 0:
-                    invert(b - 1, 1)
-                sort_next_head()
-                if b > 0:
-                    scale(b - 1, 2)
-                    scale(b - 1, 3)
-                    store(b - 1, 1)
-                if more:
-                    empty(banks[0][1], weight_place(grouped[0], 1))
-                    quantise(grouped[0], weights[b + 1], half_passes(0))
-                    empty(banks[1][0], weight_place(grouped[1], 0))
-                    empty(banks[1][1], weight_place(grouped[1], 1))
-                sort_next_head()
-                if more:
-                    quantise(grouped[1], weights[b + 1], half_passes(1))
-            if b == 0:
-                multiply(0, 2)
-                square(0, 2)
-                multiply(0, 3)
-            elif more:
-                for i in range(TOKEN_TILES):
-                    multiply(b, i)
-                    if i < 3:
-                        square(b, i)
+                empty(banks[0][1], weight_place(grouped[0], 1), nc.vector.tensor_copy)
+            if b > 0:
+                scale_and_store_pair(b - 1, 1)
+            quantise_weights(b + 1, grouped, 0)
+            for a in range(UNIT_HEADS):
+                empty(banks[1][a], weight_place(grouped[1], a))
+            if heads_to_sort:
+                sort_head(heads_to_sort[1])
+            quantise_weights(b + 1, grouped, 1)
+            for i in range(PAIR_TILES if b == 0 else 0, TOKEN_TILES):
+                multiply(b, i)
+                if i < TOKEN_TILES - 1:
+                    square(b, i)
+            if b > 0:
                 invert(b, 0)
+
         b = WEIGHT_UNITS - 1
-        multiply(b, 0, turning_bank=True)
-        square(b, 0)
-        multiply(b, 1, turning_bank=True)
-        square(b, 1)
+        square(b - 1, 3)
+        scale_and_store_pair(b - 1, 0)
+        invert(b - 1, 1)
+        scale_and_store_pair(b - 1, 1)
+        for i in range(PAIR_TILES):
+            multiply(b, i, pool=turned_pool, tag="bank")
+            square(b, i)
         invert(b, 0)
-        scale(b, 0)
-        scale(b, 1)
-        store(b, 0)
-        multiply(b, 2, turning_bank=True)
+        scale_and_store_pair(b, 0)
+        multiply(b, 2, pool=turned_pool, tag="bank")
         square(b, 2)
-        multiply(b, 3, [0], turning_bank=True)
-        square(b, 3, [0])
-        invert(b, 1, end=3)
+        multiply(b, 3, heads=[0], pool=turned_pool, tag="bank")
+        square(b, 3, heads=[0])
+        invert(b, 1, end=PAIR_PIECES - 1)
         scale(b, 2)
-        scale(b, 3, [0])
-        store(b, 1, [0])
-        multiply(b, 3, [1])
-        square(b, 3, [1])
-        invert(b, 1, first=3)
-        scale(b, 3, [1])
-        store(b, 1, [1])
+        scale(b, 3, heads=[0])
+        store(b, 1, heads=[0])
+        multiply(b, 3, heads=[1])
+        square(b, 3, heads=[1])
+        invert(b, 1, first=PAIR_PIECES - 1)
+        scale(b, 3, heads=[1])
+        store(b, 1, heads=[1])

import concourse.mybir as mybir
from concourse.masks import make_identity

F32 = mybir.dt.float32
BF16 = mybir.dt.bfloat16
U32 = mybir.dt.uint32
U8 = mybir.dt.uint8
FP8X4 = mybir.dt.float8_e4m3fn_x4
ACT = mybir.ActivationFunctionType
ALU = mybir.AluOpType

P = 128
TOKENS, EMBED, HEADS, HEAD_DIM = 512, 2048, 16, 128
EPS = 1e-05

K_PASS = 4 * P
PASSES = EMBED // K_PASS
PASS_WORDS = K_PASS // 2
HALVES = 2
HALF_PASSES = PASSES // HALVES
HALF_COLS = EMBED // HALVES

TOKEN_TILES = TOKENS // P
PAIR_TILES = 2
UNIT_HEADS = 2
UNIT_COLS = UNIT_HEADS * P
WEIGHT_UNITS = HEADS // UNIT_HEADS
PAIR_PIECES = PAIR_TILES * UNIT_HEADS

DIRECT_HEAD = 3

IDLE_AT_START = 4
IDLE_COLS = 512

SORTED_BUFS = 10
GROUPED_BUFS = 4
RESULT_BUFS = WEIGHT_UNITS * TOKEN_TILES // PAIR_TILES

FLOPS = 2 * TOKENS * EMBED * HEADS * HEAD_DIM


def tile_combcrossattention_pa_kernel(tc, hidden_states, Wq, q_norm_w, out):
    nc = tc.nc

    with (
        tc.tile_pool(name="consts", bufs=1) as consts,
        tc.tile_pool(name="raw", bufs=1) as raw_pool,
        tc.tile_pool(name="sorted", bufs=SORTED_BUFS) as sorted_pool,
        tc.tile_pool(name="quantised", bufs=1) as quantised,
        tc.tile_pool(name="grouped", bufs=GROUPED_BUFS) as grouped_pool,
        tc.tile_pool(name="stats", bufs=6) as stats,
        tc.tile_pool(name="results", bufs=RESULT_BUFS) as results,
        tc.psum_pool(name="turned", bufs=4) as turned_pool,
        tc.psum_pool(name="sums", bufs=TOKEN_TILES) as sums_pool,
        tc.manual_schedule(),
    ):
        tokens_by_partition = hidden_states.rearrange("(p i) k -> p i k", p=P)
        token_raw = []
        weight_raw = []

        def load_tokens(i, pieces=1):
            raw = raw_pool.tile([P, EMBED], BF16, name="token_raw%d" % i)
            width = EMBED // pieces
            for n in range(pieces):
                cols = slice(width * n, width * (n + 1))
                nc.sync.dma_start(out=raw[:, cols], in_=tokens_by_partition[:, i, cols])
            token_raw.append(raw)

        def load_weights(head):
            raw = raw_pool.tile([P, EMBED], BF16, name="weight_raw%d" % head)
            nc.sync.dma_start(out=raw[:], in_=Wq[P * head : P * (head + 1), :])
            weight_raw.append(raw)

        load_tokens(0, pieces=HALVES)
        load_weights(0)
        load_weights(1)
        for i in range(1, TOKEN_TILES):
            load_tokens(i)
        for head in range(2, HEADS):
            load_weights(head)

        identity = consts.tile([P, P], F32)
        make_identity(nc, identity[:])
        ones = consts.tile([P, P], BF16)
        nc.vector.memset(ones[:], 1.0)
        idle_rhs = consts.tile([P, IDLE_COLS], BF16)
        nc.vector.memset(idle_rhs[:], 0.0)
        gain_row = consts.tile([P, HEAD_DIM], BF16)
        nc.vector.memset(gain_row[:], 0.0)
        nc.scalar.dma_start(out=gain_row[0:1, :], in_=q_norm_w.unsqueeze(0))
        gain = consts.tile([P, HEAD_DIM], F32)
        eps = consts.tile([P, 1], F32)
        nc.vector.memset(eps[:], EPS)

        table_warmer = consts.tile([P, 1], F32)
        nc.scalar.activation(out=table_warmer[:], in_=eps[:], func=ACT.Abs_reciprocal_sqrt)

        def keep_clock_up(count):
            unread = sums_pool.tile([P, IDLE_COLS], F32, name="unread", tag="q")
            for n in range(count):
                nc.tensor.matmul(out=unread[:], lhsT=ones[:], rhs=idle_rhs[:], start=True, stop=True)

        def spread_gain():
            bank = turned_pool.tile([P, 4, P], F32, name="bank")
            nc.tensor.matmul(out=bank[:, 0, :], lhsT=ones[:], rhs=gain_row[:], start=True, stop=True)
            nc.vector.tensor_copy(out=gain[:], in_=bank[:, 0, :])

        def sort(raw):
            halves = []
            for h in range(HALVES):
                words = sorted_pool.tile([P, 2, HALF_COLS // 4], F32, name="words")
                half = raw[:, HALF_COLS * h : HALF_COLS * (h + 1)].bitcast(F32)
                nc.vector.tensor_copy(out=words[:], in_=half.rearrange("p (w u) -> p u w", u=2))
                halves.append(words)
            return halves

        def turn_half(raw, words, h):
            bank = turned_pool.tile([P, 4, P], F32, name="bank")
            for n in range(HALF_PASSES):
                for u in range(2):
                    if words is None:
                        first = PASS_WORDS * (HALF_PASSES * h + n) + u
                        source = raw[:].bitcast(F32)[:, first : first + PASS_WORDS - 1 : 2]
                    else:
                        source = words[h][:, u, P * n : P * (n + 1)]
                    nc.tensor.transpose(bank[:, 2 * n + u, :], source, identity[:])
            return bank

        def turn(raw, words=None):
            return [turn_half(raw, words, h) for h in range(HALVES)]

        def new_operand(name, tiles):
            codes = quantised.tile([P, PASSES, tiles * P], U32, name=name + "_codes", align_bytes=64)
            scales = quantised.tile([P, PASSES, tiles * P], U8, name=name + "_scales", align_bytes=64)
            return codes, scales

        def new_grouped():
            return grouped_pool.tile([P, 4 * P * 4], BF16, name="grouped", align_bytes=64)

        def empty(bank, target, copy=nc.scalar.copy):
            copy(out=target, in_=bank[:].rearrange("p (g u) c -> p g c u", u=2))

        def weight_place(grouped, a):
            return grouped[:].bitcast(F32).rearrange(
                "p (g a c u) -> p g a c u", g=HALF_PASSES, a=UNIT_HEADS, u=2
            )[:, :, a]

        def empty_token_banks(banks):
            grouped = new_grouped()
            places = grouped[:].bitcast(F32).rearrange(
                "p (h g c u) -> p h g c u", h=HALVES, g=HALF_PASSES, u=2
            )
            for h in range(HALVES):
                empty(banks[h], places[:, h])
            return grouped

        def quantise(grouped, operand, first_pass, end_pass):
            codes, scales = operand
            nc.vector.quantize_mx(
                out=codes[:, first_pass:end_pass, :].rearrange("p g n -> p (g n)").bitcast(FP8X4),
                scales=scales[:, first_pass:end_pass, :].rearrange("p g n -> p (g n)"),
                in_=grouped[:],
            )

        def quantise_tokens(i, grouped):
            tokens.append(new_operand("token%d" % i, 1))
            quantise(grouped, tokens[i], 0, PASSES)

        def quantise_weights(b, grouped, h):
            quantise(grouped[h], weights[b], HALF_PASSES * h, HALF_PASSES * (h + 1))

        sorted_heads = {}

        def sort_head(head):
            sorted_heads[head] = None if head == DIRECT_HEAD else sort(weight_raw[head])

        def multiply(b, i, heads=range(UNIT_HEADS), pool=sums_pool, tag="q"):
            weight_codes, weight_scales = weights[b]
            token_codes, token_scales = tokens[i]
            cols = slice(P * heads[0], P * (heads[-1] + 1))
            bank = pool.tile([P, 4, P], F32, name="q", tag=tag)
            q = bank[:, 0 : len(heads), :].rearrange("p h d -> p (h d)")
            for g in range(PASSES):
                nc.tensor.matmul_mx(
                    out=q,
                    lhsT=token_codes[:, g, :].bitcast(FP8X4),
                    lhsT_scale=token_scales[:, g, :],
                    rhs=weight_codes[:, g, cols].bitcast(FP8X4),
                    rhs_scale=weight_scales[:, g, cols],
                    start=(g == 0),
                    stop=(g == PASSES - 1),
                )
            for n, h in enumerate(heads):
                sums[b, i, h] = bank[:, n, :]

        def piece(i, h):
            return UNIT_HEADS * (i % PAIR_TILES) + h

        def square(b, i, heads=range(UNIT_HEADS)):
            pair = b, i // PAIR_TILES
            if pair not in sum_squares:
                sum_squares[pair] = stats.tile([P, PAIR_PIECES], F32, name="sum_squares")
                inv_rms[pair] = stats.tile([P, PAIR_PIECES], F32, name="inv_rms")
                outcome[pair] = results.tile([P, UNIT_HEADS, PAIR_TILES, HEAD_DIM], F32, name="result")
            squares = stats.tile([P, UNIT_HEADS, HEAD_DIM], F32, name="squares")
            for h in heads:
                n = piece(i, h)
                nc.scalar.activation(
                    out=squares[:, h, :],
                    in_=sums[b, i, h],
                    func=ACT.Square,
                    accum_out=sum_squares[pair][:, n : n + 1],
                )

        def invert(b, r, first=0, end=PAIR_PIECES):
            nc.scalar.activation(
                out=inv_rms[b, r][:, first:end],
                in_=sum_squares[b, r][:, first:end],
                func=ACT.Abs_reciprocal_sqrt,
                scale=1.0 / HEAD_DIM,
                bias=eps[:],
            )

        def scale(b, i, heads=range(UNIT_HEADS)):
            pair = b, i // PAIR_TILES
            for h in heads:
                n = piece(i, h)
                nc.vector.scalar_tensor_tensor(
                    out=outcome[pair][:, h, i % PAIR_TILES, :],
                    in0=sums[b, i, h],
                    scalar=inv_rms[pair][:, n : n + 1],
                    in1=gain[:],
                    op0=ALU.mult,
                    op1=ALU.mult,
                )

        out_by_partition = out.rearrange("h (p i) d -> p h i d", p=P)

        def store(b, r, heads=range(UNIT_HEADS)):
            nc.sync.dma_start(
                out=out_by_partition[
                    :,
                    UNIT_HEADS * b + heads[0] : UNIT_HEADS * b + heads[-1] + 1,
                    PAIR_TILES * r : PAIR_TILES * (r + 1),
                    :,
                ],
                in_=outcome[b, r][:, heads[0] : heads[-1] + 1],
            )

        def scale_and_store_pair(b, r):
            for i in range(PAIR_TILES * r, PAIR_TILES * (r + 1)):
                scale(b, i)
            store(b, r)

        tokens, weights = [], []
        sums, sum_squares, inv_rms, outcome = {}, {}, {}, {}

        keep_clock_up(IDLE_AT_START)
        weights.append(new_operand("weight0", UNIT_HEADS))
        grouped = [new_grouped() for h in range(HALVES)]
        banks = turn(token_raw[0], sort(token_raw[0]))
        keep_clock_up(2)
        grouped_tokens = [empty_token_banks(banks)]
        banks = turn(weight_raw[0], sort(weight_raw[0]))
        keep_clock_up(2)
        for h in range(HALVES):
            empty(banks[h], weight_place(grouped[h], 0))
        words = sort(weight_raw[1])
        quantise_tokens(0, grouped_tokens[0])
        banks = turn(weight_raw[1], words)
        keep_clock_up(1)
        for h in range(HALVES):
            empty(banks[h], weight_place(grouped[h], 1))
        banks = turn(token_raw[1])
        keep_clock_up(1)
        grouped_tokens.append(empty_token_banks(banks))
        banks = turn(token_raw[2])
        for h in range(HALVES):
            quantise_weights(0, grouped, h)
        spread_gain()
        multiply(0, 0)
        grouped_tokens.append(empty_token_banks(banks))
        banks = turn(token_raw[3])
        quantise_tokens(1, grouped_tokens[1])
        square(0, 0)
        multiply(0, 1)
        grouped_tokens.append(empty_token_banks(banks))
        sort_head(2)
        quantise_tokens(2, grouped_tokens[2])
        square(0, 1)
        sort_head(3)
        quantise_tokens(3, grouped_tokens[3])
        invert(0, 0)
        scale_and_store_pair(0, 0)

        for b in range(WEIGHT_UNITS - 1):
            heads_to_sort = range(UNIT_HEADS * (b + 2), min(UNIT_HEADS * (b + 3), HEADS))
            weights.append(new_operand("weight%d" % (b + 1), UNIT_HEADS))
            banks = [
                [turn_half(weight_raw[head], sorted_heads[head], h) for head in (2 * b + 2, 2 * b + 3)]
                for h in range(HALVES)
            ]
            grouped = [new_grouped() for h in range(HALVES)]
            if b > 0:
                square(b - 1, 3)
                if b > 1:
                    scale_and_store_pair(b - 1, 0)
            empty(banks[0][0], weight_place(grouped[0], 0))
            if b > 0:
                invert(b - 1, 1)
            if heads_to_sort:
                sort_head(heads_to_sort[0])
                empty(banks[0][1], weight_place(grouped[0], 1))
            else:
                empty(banks[0][1], weight_place(grouped[0], 1), nc.vector.tensor_copy)
            if b > 0:
                scale_and_store_pair(b - 1, 1)
            quantise_weights(b + 1, grouped, 0)
            for a in range(UNIT_HEADS):
                empty(banks[1][a], weight_place(grouped[1], a))
            if heads_to_sort:
                sort_head(heads_to_sort[1])
            quantise_weights(b + 1, grouped, 1)
            for i in range(PAIR_TILES if b == 0 else 0, TOKEN_TILES):
                multiply(b, i)
                if i < TOKEN_TILES - 1:
                    square(b, i)
            if b > 0:
                invert(b, 0)

        b = WEIGHT_UNITS - 1
        square(b - 1, 3)
        scale_and_store_pair(b - 1, 0)
        invert(b - 1, 1)
        scale_and_store_pair(b - 1, 1)
        for i in range(PAIR_TILES):
            multiply(b, i, pool=turned_pool, tag="bank")
            square(b, i)
        invert(b, 0)
        scale_and_store_pair(b, 0)
        multiply(b, 2, pool=turned_pool, tag="bank")
        square(b, 2)
        multiply(b, 3, heads=[0], pool=turned_pool, tag="bank")
        square(b, 3, heads=[0])
        invert(b, 1, end=PAIR_PIECES - 1)
        scale(b, 2)
        scale(b, 3, heads=[0])
        store(b, 1, heads=[0])
        multiply(b, 3, heads=[1])
        square(b, 3, heads=[1])
        invert(b, 1, first=PAIR_PIECES - 1)
        scale(b, 3, heads=[1])
        store(b, 1, heads=[1])
